import numpy as np
import ml_dtypes


def mxq(x, axis, fmt="e4m3"):
    dtype, down = {"e4m3": (ml_dtypes.float8_e4m3fn, 7), "e5m2": (ml_dtypes.float8_e5m2, 14)}[fmt]
    v = np.moveaxis(np.asarray(x, np.float32).astype(ml_dtypes.bfloat16).astype(np.float64), axis, -1)
    blocks = v.reshape(v.shape[:-1] + (-1, 32))
    amax = np.abs(blocks).max(-1, keepdims=True)
    byte = np.maximum(np.where(amax > 0, np.frexp(amax)[1] - 1 + 127, 0) - down, 1)
    scale = np.exp2(byte - 127.0)
    codes = (blocks / scale).astype(np.float32).astype(dtype).astype(np.float64)
    return np.moveaxis((codes * scale).reshape(v.shape), -1, axis)


WIDE = False


def mx_kscale(k):
    if not WIDE:
        return np.ones(k)
    levels = np.array([10, -10, 5, -5, 0])
    a = np.random.permutation(np.resize(levels, k // 512 * 4)).reshape(k // 512, 4)
    idx = np.arange(k)
    return np.exp2(a[idx // 512, idx % 128 // 32])


BF16 = ml_dtypes.bfloat16


def bf(x):
    return np.asarray(x, np.float32).astype(BF16)


def f64(x):
    return np.asarray(x).astype(np.float64)


B, S, D, N, A, F = 64, 64, 512, 128, 128, 512
LN_EPS = 1e-5


def setup_inputs():
    t = mx_kscale(F)
    return {
        "actions": bf(np.random.standard_normal((B, N, A))),
        "W_ae": bf(np.random.standard_normal((F, A)) / np.sqrt(A)),
        "b_ae": bf(np.random.standard_normal(F) * 0.4),
        "ln_g": bf((1.0 + 0.1 * np.random.standard_normal(F)) * t),
        "ln_b": bf(0.2 * np.random.standard_normal(F) * t),
        "Wv": bf(np.random.standard_normal((F, F)) / np.sqrt(F) / t[None, :]),
    }


def reference(actions, W_ae, b_ae, ln_g, ln_b, Wv):
    a = f64(actions) @ f64(W_ae).T + f64(b_ae)
    mu = a.mean(-1, keepdims=True)
    var = ((a - mu) ** 2).mean(-1, keepdims=True)
    a_n = (a - mu) / np.sqrt(var + LN_EPS) * f64(ln_g) + f64(ln_b)
    a_n = a_n
    return mxq(a_n, 2, "e4m3") @ mxq(f64(Wv), 1, "e4m3").T

@@ -1,0 +1,191 @@
+from contextlib import ExitStack
+
+import concourse.mybir as mybir
+from concourse.masks import make_identity
+
+BF16 = mybir.dt.bfloat16
+F32 = mybir.dt.float32
+U32 = mybir.dt.uint32
+U8 = mybir.dt.uint8
+FP8X4 = mybir.dt.float8_e4m3fn_x4
+ACT = mybir.ActivationFunctionType
+ALU = mybir.AluOpType
+
+P = 128
+PACK = 4
+TOKENS = 64 * 128
+A = 128
+F = 512
+O = 512
+TILES = TOKENS // P
+GROUP = 4
+GROUPS = TILES // GROUP
+GROUP_TOKENS = GROUP * P
+LOAD_CHUNKS = 4
+LN_EPS = 1e-5
+
+FLOPS = 2 * TOKENS * A * F + 2 * TOKENS * F * O
+
+
+def block(i):
+    return slice(i * P, (i + 1) * P)
+
+
+def tile_actionbindingattention_pa_kernel(tc, actions, W_ae, b_ae, ln_g, ln_b, Wv, out):
+    nc = tc.nc
+    x_dram = actions.flatten_outer_dims().rearrange("(p n) a -> p n a", n=TILES)
+    out_dram = out.flatten_outer_dims().rearrange("(p n) o -> p n o", n=TILES)
+
+    with ExitStack() as ctx:
+        keep = ctx.enter_context(tc.tile_pool(name="keep", bufs=1))
+        work = ctx.enter_context(tc.tile_pool(name="work", bufs=3))
+        small = ctx.enter_context(tc.tile_pool(name="small", bufs=4))
+        ps_bf = ctx.enter_context(tc.psum_pool(name="ps_bf", bufs=1))
+        ps_a = ctx.enter_context(tc.psum_pool(name="ps_a", bufs=2))
+        ps_z = ctx.enter_context(tc.psum_pool(name="ps_z", bufs=3))
+        ps_o = ctx.enter_context(tc.psum_pool(name="ps_o", bufs=2))
+
+        w_ae_sb = keep.tile([P, PACK, A], BF16)
+        nc.sync.dma_start(out=w_ae_sb[:], in_=W_ae.rearrange("(j p) a -> p j a", p=P))
+        x_all = keep.tile([P, TILES, A], BF16)
+        chunk = TILES // LOAD_CHUNKS
+        nc.sync.dma_start(out=x_all[:, 0:chunk, :], in_=x_dram[:, 0:chunk, :])
+        bias_bc = keep.tile([P, F], BF16)
+        nc.sync.dma_start(out=bias_bc[:], in_=b_ae.partition_broadcast(P))
+        gain_shift_rows = keep.tile([P, P], BF16)
+        nc.vector.memset(gain_shift_rows[:], 0.0)
+        nc.sync.dma_start(out=gain_shift_rows[0:PACK, :], in_=ln_g.rearrange("(j p) -> j p", p=P))
+        nc.sync.dma_start(out=gain_shift_rows[PACK : 2 * PACK, :], in_=ln_b.rearrange("(j p) -> j p", p=P))
+        wv_sb = keep.tile([P, O // P, F], BF16)
+        nc.sync.dma_start(out=wv_sb[:], in_=Wv.rearrange("(b r) f -> r b f", r=P))
+        for c in range(1, LOAD_CHUNKS):
+            rows = slice(c * chunk, (c + 1) * chunk)
+            nc.sync.dma_start(out=x_all[:, rows, :], in_=x_dram[:, rows, :])
+
+        ident_bf = keep.tile([P, P], BF16)
+        make_identity(nc, ident_bf[:])
+        ident_f32 = keep.tile([P, P], F32)
+        make_identity(nc, ident_f32[:])
+        eps = keep.tile([P, 1], F32)
+        nc.vector.memset(eps[:], LN_EPS)
+
+        w_aeT_ps = ps_bf.tile([P, F], BF16, tag="bf")
+        for j in range(PACK):
+            nc.tensor.transpose(out=w_aeT_ps[:, block(j)], in_=w_ae_sb[:, j, :], identity=ident_bf[:])
+        w_aeT = keep.tile([P, F], BF16)
+        nc.vector.tensor_copy(out=w_aeT[:], in_=w_aeT_ps[:])
+
+        gain_shift_ps = ps_bf.tile([P, P], BF16, tag="bf")
+        nc.tensor.transpose(out=gain_shift_ps[:], in_=gain_shift_rows[:], identity=ident_bf[:])
+        gain = keep.tile([P, PACK], F32)
+        nc.vector.tensor_copy(out=gain[:], in_=gain_shift_ps[:, 0:PACK])
+        shift = keep.tile([P, PACK], F32)
+        nc.vector.tensor_copy(out=shift[:], in_=gain_shift_ps[:, PACK : 2 * PACK])
+
+        wv_grouped = keep.tile([P, O, PACK], BF16, align_bytes=64)
+        for b in range(O // P):
+            wvT_ps = ps_bf.tile([P, PACK, P], BF16, tag="bf")
+            for j in range(PACK):
+                nc.tensor.transpose(out=wvT_ps[:, j, :], in_=wv_sb[:, b, block(j)], identity=ident_bf[:])
+            nc.vector.tensor_copy(out=wv_grouped[:, block(b), :], in_=wvT_ps[:].rearrange("p j o -> p o j"))
+        wv_codes = keep.tile([P, O], U32, align_bytes=64)
+        wv_scales = keep.tile([P, O], U8, align_bytes=64)
+        nc.vector.quantize_mx(
+            out=wv_codes[:].bitcast(FP8X4),
+            scales=wv_scales[:],
+            in_=wv_grouped[:].rearrange("p o j -> p (o j)"),
+        )
+
+        for g in range(GROUPS):
+            xT_ps = ps_bf.tile([P, GROUP_TOKENS], BF16, tag="bf")
+            for n in range(GROUP):
+                nc.tensor.transpose(out=xT_ps[:, block(n)], in_=x_all[:, g * GROUP + n, :], identity=ident_bf[:])
+            xT = work.tile([P, GROUP_TOKENS], BF16)
+            nc.scalar.copy(out=xT[:], in_=xT_ps[:])
+
+            a_sb = work.tile([P, GROUP, F], F32)
+            a_sum = small.tile([P, GROUP], F32)
+            for n in range(GROUP):
+                a_ps = ps_a.tile([P, F], F32)
+                nc.tensor.matmul(out=a_ps[:], lhsT=xT[:, block(n)], rhs=w_aeT[:], start=True, stop=True)
+                nc.vector.scalar_tensor_tensor(
+                    out=a_sb[:, n, :],
+                    in0=a_ps[:],
+                    scalar=1.0,
+                    in1=bias_bc[:],
+                    op0=ALU.mult,
+                    op1=ALU.add,
+                    accum_out=a_sum[:, n : n + 1],
+                )
+
+            neg_mean = small.tile([P, GROUP], F32)
+            nc.vector.tensor_scalar_mul(out=neg_mean[:], in0=a_sum[:], scalar1=-1.0 / F)
+            dev_sq_sum = small.tile([P, GROUP], F32)
+            for n in range(GROUP):
+                dev_sq = work.tile([P, F], BF16)
+                nc.scalar.activation(
+                    out=dev_sq[:],
+                    in_=a_sb[:, n, :],
+                    func=ACT.Square,
+                    bias=neg_mean[:, n : n + 1],
+                    scale=1.0,
+                    accum_out=dev_sq_sum[:, n : n + 1],
+                )
+            std = small.tile([P, GROUP], F32)
+            nc.scalar.activation(out=std[:], in_=dev_sq_sum[:], func=ACT.Sqrt, bias=eps[:], scale=1.0 / F)
+            rstd = small.tile([P, GROUP], F32)
+            nc.vector.reciprocal(out=rstd[:], in_=std[:])
+            neg_mean_rstd = small.tile([P, GROUP], F32)
+            nc.vector.tensor_mul(out=neg_mean_rstd[:], in0=neg_mean[:], in1=rstd[:])
+
+            z_sb = work.tile([P, GROUP, F], F32)
+            for n in range(GROUP):
+                nc.gpsimd.tensor_scalar(
+                    out=z_sb[:, n, :],
+                    in0=a_sb[:, n, :],
+                    scalar1=rstd[:, n : n + 1],
+                    scalar2=neg_mean_rstd[:, n : n + 1],
+                    op0=ALU.mult,
+                    op1=ALU.add,
+                )
+
+            a_n_planes = work.tile([P, PACK, GROUP_TOKENS], BF16)
+            for j in range(PACK):
+                zT_ps = ps_z.tile([P, GROUP_TOKENS], F32)
+                for n in range(GROUP):
+                    nc.tensor.transpose(out=zT_ps[:, block(n)], in_=z_sb[:, n, block(j)], identity=ident_f32[:])
+                nc.scalar.activation(
+                    out=a_n_planes[:, j, :],
+                    in_=zT_ps[:],
+                    func=ACT.Identity,
+                    scale=gain[:, j : j + 1],
+                    bias=shift[:, j : j + 1],
+                )
+
+            a_n_grouped = work.tile([P, GROUP_TOKENS, PACK], BF16, align_bytes=64)
+            nc.vector.tensor_copy(out=a_n_grouped[:], in_=a_n_planes[:].rearrange("p j c -> p c j"))
+            a_n_codes = work.tile([P, GROUP_TOKENS], U32, align_bytes=64)
+            a_n_scales = work.tile([P, GROUP_TOKENS], U8, align_bytes=64)
+            nc.vector.quantize_mx(
+                out=a_n_codes[:].bitcast(FP8X4),
+                scales=a_n_scales[:],
+                in_=a_n_grouped[:].rearrange("p c j -> p (c j)"),
+            )
+
+            out_sb = work.tile([P, GROUP, O], F32)
+            for n in range(GROUP):
+                out_ps = ps_o.tile([P, O], F32)
+                nc.tensor.matmul_mx(
+                    out=out_ps[:],
+                    lhsT=a_n_codes[:, block(n)].bitcast(FP8X4),
+                    lhsT_scale=a_n_scales[:, block(n)],
+                    rhs=wv_codes[:].bitcast(FP8X4),
+                    rhs_scale=wv_scales[:],
+                    start=True,
+                    stop=True,
+                )
+                if n % 2 == 0:
+                    nc.vector.tensor_copy(out=out_sb[:, n, :], in_=out_ps[:])
+                else:
+                    nc.scalar.copy(out=out_sb[:, n, :], in_=out_ps[:])
+            nc.sync.dma_start(out=out_dram[:, g * GROUP : (g + 1) * GROUP, :], in_=out_sb[:])

@@ -22,13 +22,35 @@ GROUP = 4
 GROUPS = TILES // GROUP
 GROUP_TOKENS = GROUP * P
 LOAD_CHUNKS = 4
+RUN = 4
 LN_EPS = 1e-5
+
+SQUARE_LAG = 2
+DEVIATION_LAG = SQUARE_LAG + GROUP - 1
+NORMALISE_LAG = 6
+FLIP_LAG = 10
+REGROUP_LAG = 15
+QUANTISE_LAG = 16
+PROJECT_LAG = 17
+STEPS = TILES + PROJECT_LAG
+SCALAR_BANK = 2
+PREPARE_STEP = 4
 
 FLOPS = 2 * TOKENS * A * F + 2 * TOKENS * F * O
 
 
 def block(i):
     return slice(i * P, (i + 1) * P)
+
+
+def tile_due(step, lag):
+    k = step - lag
+    return divmod(k, GROUP) if 0 <= k < TILES else None
+
+
+def group_due(step, lag):
+    due = tile_due(step, lag)
+    return due[0] if due is not None and due[1] == 0 else None
 
 
 def tile_actionbindingattention_pa_kernel(tc, actions, W_ae, b_ae, ln_g, ln_b, Wv, out):
@@ -40,10 +62,11 @@ def tile_actionbindingattention_pa_kernel(tc, actions, W_ae, b_ae, ln_g, ln_b, W
         keep = ctx.enter_context(tc.tile_pool(name="keep", bufs=1))
         work = ctx.enter_context(tc.tile_pool(name="work", bufs=3))
         small = ctx.enter_context(tc.tile_pool(name="small", bufs=4))
-        ps_bf = ctx.enter_context(tc.psum_pool(name="ps_bf", bufs=1))
+        ps_bf = ctx.enter_context(tc.psum_pool(name="ps_bf", bufs=2))
         ps_a = ctx.enter_context(tc.psum_pool(name="ps_a", bufs=2))
-        ps_z = ctx.enter_context(tc.psum_pool(name="ps_z", bufs=3))
+        ps_z = ctx.enter_context(tc.psum_pool(name="ps_z", bufs=2))
         ps_o = ctx.enter_context(tc.psum_pool(name="ps_o", bufs=2))
+        ctx.enter_context(tc.manual_schedule())
 
         w_ae_sb = keep.tile([P, PACK, A], BF16)
         nc.sync.dma_start(out=w_ae_sb[:], in_=W_ae.rearrange("(j p) a -> p j a", p=P))
@@ -75,117 +98,188 @@ def tile_actionbindingattention_pa_kernel(tc, actions, W_ae, b_ae, ln_g, ln_b, W
         w_aeT = keep.tile([P, F], BF16)
         nc.vector.tensor_copy(out=w_aeT[:], in_=w_aeT_ps[:])
 
-        gain_shift_ps = ps_bf.tile([P, P], BF16, tag="bf")
-        nc.tensor.transpose(out=gain_shift_ps[:], in_=gain_shift_rows[:], identity=ident_bf[:])
         gain = keep.tile([P, PACK], F32)
-        nc.vector.tensor_copy(out=gain[:], in_=gain_shift_ps[:, 0:PACK])
         shift = keep.tile([P, PACK], F32)
-        nc.vector.tensor_copy(out=shift[:], in_=gain_shift_ps[:, PACK : 2 * PACK])
-
         wv_grouped = keep.tile([P, O, PACK], BF16, align_bytes=64)
-        for b in range(O // P):
+        wv_codes = keep.tile([P, O], U32, align_bytes=64)
+        wv_scales = keep.tile([P, O], U8, align_bytes=64)
+
+        def transpose_gain_shift():
+            gain_shift_ps = ps_bf.tile([P, P], BF16, tag="bf")
+            nc.tensor.transpose(out=gain_shift_ps[:], in_=gain_shift_rows[:], identity=ident_bf[:])
+            nc.vector.tensor_copy(out=gain[:], in_=gain_shift_ps[:, 0:PACK])
+            nc.vector.tensor_copy(out=shift[:], in_=gain_shift_ps[:, PACK : 2 * PACK])
+
+        def transpose_wv(b):
             wvT_ps = ps_bf.tile([P, PACK, P], BF16, tag="bf")
             for j in range(PACK):
                 nc.tensor.transpose(out=wvT_ps[:, j, :], in_=wv_sb[:, b, block(j)], identity=ident_bf[:])
             nc.vector.tensor_copy(out=wv_grouped[:, block(b), :], in_=wvT_ps[:].rearrange("p j o -> p o j"))
-        wv_codes = keep.tile([P, O], U32, align_bytes=64)
-        wv_scales = keep.tile([P, O], U8, align_bytes=64)
-        nc.vector.quantize_mx(
-            out=wv_codes[:].bitcast(FP8X4),
-            scales=wv_scales[:],
-            in_=wv_grouped[:].rearrange("p o j -> p (o j)"),
-        )
 
-        for g in range(GROUPS):
+        def quantise_wv():
+            nc.vector.quantize_mx(
+                out=wv_codes[:].bitcast(FP8X4),
+                scales=wv_scales[:],
+                in_=wv_grouped[:].rearrange("p o j -> p (o j)"),
+            )
+
+        xT, a_sb, a_sum, dev_sq_sum, std, z_sb = {}, {}, {}, {}, {}, {}
+        a_n_planes, a_n_grouped, a_n_codes, a_n_scales, out_sb = {}, {}, {}, {}, {}
+
+        def transpose_actions(g):
             xT_ps = ps_bf.tile([P, GROUP_TOKENS], BF16, tag="bf")
             for n in range(GROUP):
                 nc.tensor.transpose(out=xT_ps[:, block(n)], in_=x_all[:, g * GROUP + n, :], identity=ident_bf[:])
-            xT = work.tile([P, GROUP_TOKENS], BF16)
-            nc.scalar.copy(out=xT[:], in_=xT_ps[:])
+            xT_sb = work.tile([P, GROUP_TOKENS], BF16)
+            nc.scalar.copy(out=xT_sb[:], in_=xT_ps[:])
+            xT[g] = xT_sb
 
-            a_sb = work.tile([P, GROUP, F], F32)
-            a_sum = small.tile([P, GROUP], F32)
-            for n in range(GROUP):
-                a_ps = ps_a.tile([P, F], F32)
-                nc.tensor.matmul(out=a_ps[:], lhsT=xT[:, block(n)], rhs=w_aeT[:], start=True, stop=True)
-                nc.vector.scalar_tensor_tensor(
-                    out=a_sb[:, n, :],
-                    in0=a_ps[:],
-                    scalar=1.0,
-                    in1=bias_bc[:],
-                    op0=ALU.mult,
-                    op1=ALU.add,
-                    accum_out=a_sum[:, n : n + 1],
-                )
+        def encode(g, n):
+            if n == 0:
+                a_tile = work.tile([P, GROUP, F], F32)
+                a_sb[g] = a_tile
+                sum_tile = small.tile([P, GROUP], F32)
+                a_sum[g] = sum_tile
+            a_ps = ps_a.tile([P, F], F32)
+            nc.tensor.matmul(out=a_ps[:], lhsT=xT[g][:, block(n)], rhs=w_aeT[:], start=True, stop=True)
+            nc.vector.scalar_tensor_tensor(
+                out=a_sb[g][:, n, :],
+                in0=a_ps[:],
+                scalar=1.0,
+                in1=bias_bc[:],
+                op0=ALU.mult,
+                op1=ALU.add,
+                accum_out=a_sum[g][:, n : n + 1],
+            )
 
-            neg_mean = small.tile([P, GROUP], F32)
-            nc.vector.tensor_scalar_mul(out=neg_mean[:], in0=a_sum[:], scalar1=-1.0 / F)
-            dev_sq_sum = small.tile([P, GROUP], F32)
-            for n in range(GROUP):
-                dev_sq = work.tile([P, F], BF16)
-                nc.scalar.activation(
-                    out=dev_sq[:],
-                    in_=a_sb[:, n, :],
-                    func=ACT.Square,
-                    bias=neg_mean[:, n : n + 1],
-                    scale=1.0,
-                    accum_out=dev_sq_sum[:, n : n + 1],
-                )
-            std = small.tile([P, GROUP], F32)
-            nc.scalar.activation(out=std[:], in_=dev_sq_sum[:], func=ACT.Sqrt, bias=eps[:], scale=1.0 / F)
+        def square(g, n):
+            if n == 0:
+                sq_tile = small.tile([P, GROUP], F32)
+                dev_sq_sum[g] = sq_tile
+            dev_sq = work.tile([P, F], BF16)
+            nc.scalar.activation(
+                out=dev_sq[:],
+                in_=a_sb[g][:, n, :],
+                func=ACT.Square,
+                bias=a_sum[g][:, n : n + 1],
+                scale=-1.0 * F,
+                accum_out=dev_sq_sum[g][:, n : n + 1],
+            )
+
+        def deviation(g):
+            std_tile = small.tile([P, GROUP], F32)
+            nc.scalar.activation(
+                out=std_tile[:], in_=dev_sq_sum[g][:], func=ACT.Sqrt, bias=eps[:], scale=1.0 / (F * F * F)
+            )
+            std[g] = std_tile
+
+        def normalise(g):
             rstd = small.tile([P, GROUP], F32)
-            nc.vector.reciprocal(out=rstd[:], in_=std[:])
+            nc.vector.reciprocal(out=rstd[:], in_=std[g][:])
             neg_mean_rstd = small.tile([P, GROUP], F32)
-            nc.vector.tensor_mul(out=neg_mean_rstd[:], in0=neg_mean[:], in1=rstd[:])
-
-            z_sb = work.tile([P, GROUP, F], F32)
+            nc.vector.scalar_tensor_tensor(
+                out=neg_mean_rstd[:], in0=a_sum[g][:], scalar=-1.0 / F, in1=rstd[:], op0=ALU.mult, op1=ALU.mult
+            )
+            z_tile = work.tile([P, GROUP, F], F32)
             for n in range(GROUP):
                 nc.gpsimd.tensor_scalar(
-                    out=z_sb[:, n, :],
-                    in0=a_sb[:, n, :],
+                    out=z_tile[:, n, :],
+                    in0=a_sb[g][:, n, :],
                     scalar1=rstd[:, n : n + 1],
                     scalar2=neg_mean_rstd[:, n : n + 1],
                     op0=ALU.mult,
                     op1=ALU.add,
                 )
+            z_sb[g] = z_tile
 
-            a_n_planes = work.tile([P, PACK, GROUP_TOKENS], BF16)
-            for j in range(PACK):
-                zT_ps = ps_z.tile([P, GROUP_TOKENS], F32)
-                for n in range(GROUP):
-                    nc.tensor.transpose(out=zT_ps[:, block(n)], in_=z_sb[:, n, block(j)], identity=ident_f32[:])
-                nc.scalar.activation(
-                    out=a_n_planes[:, j, :],
-                    in_=zT_ps[:],
-                    func=ACT.Identity,
-                    scale=gain[:, j : j + 1],
-                    bias=shift[:, j : j + 1],
-                )
-
-            a_n_grouped = work.tile([P, GROUP_TOKENS, PACK], BF16, align_bytes=64)
-            nc.vector.tensor_copy(out=a_n_grouped[:], in_=a_n_planes[:].rearrange("p j c -> p c j"))
-            a_n_codes = work.tile([P, GROUP_TOKENS], U32, align_bytes=64)
-            a_n_scales = work.tile([P, GROUP_TOKENS], U8, align_bytes=64)
-            nc.vector.quantize_mx(
-                out=a_n_codes[:].bitcast(FP8X4),
-                scales=a_n_scales[:],
-                in_=a_n_grouped[:].rearrange("p c j -> p (c j)"),
+        def flip(g, j):
+            if j == 0:
+                planes_tile = work.tile([P, PACK, GROUP_TOKENS], BF16)
+                a_n_planes[g] = planes_tile
+            zT_ps = ps_z.tile([P, GROUP_TOKENS], F32)
+            for n in range(GROUP):
+                nc.tensor.transpose(out=zT_ps[:, block(n)], in_=z_sb[g][:, n, block(j)], identity=ident_f32[:])
+            nc.scalar.activation(
+                out=a_n_planes[g][:, j, :],
+                in_=zT_ps[:],
+                func=ACT.Identity,
+                scale=gain[:, j : j + 1],
+                bias=shift[:, j : j + 1],
             )
 
-            out_sb = work.tile([P, GROUP, O], F32)
-            for n in range(GROUP):
-                out_ps = ps_o.tile([P, O], F32)
-                nc.tensor.matmul_mx(
-                    out=out_ps[:],
-                    lhsT=a_n_codes[:, block(n)].bitcast(FP8X4),
-                    lhsT_scale=a_n_scales[:, block(n)],
-                    rhs=wv_codes[:].bitcast(FP8X4),
-                    rhs_scale=wv_scales[:],
-                    start=True,
-                    stop=True,
-                )
-                if n % 2 == 0:
-                    nc.vector.tensor_copy(out=out_sb[:, n, :], in_=out_ps[:])
-                else:
-                    nc.scalar.copy(out=out_sb[:, n, :], in_=out_ps[:])
-            nc.sync.dma_start(out=out_dram[:, g * GROUP : (g + 1) * GROUP, :], in_=out_sb[:])
+        def regroup(g):
+            grouped_tile = work.tile([P, GROUP_TOKENS, PACK], BF16, align_bytes=64)
+            nc.vector.tensor_copy(
+                out=grouped_tile[:].rearrange("p (c i) j -> p c j i", i=RUN),
+                in_=a_n_planes[g][:].rearrange("p j (c i) -> p c j i", i=RUN),
+            )
+            a_n_grouped[g] = grouped_tile
+
+        def quantise(g):
+            codes_tile = work.tile([P, GROUP_TOKENS], U32, align_bytes=64)
+            scales_tile = work.tile([P, GROUP_TOKENS], U8, align_bytes=64)
+            nc.vector.quantize_mx(
+                out=codes_tile[:].bitcast(FP8X4),
+                scales=scales_tile[:],
+                in_=a_n_grouped[g][:].rearrange("p c j -> p (c j)"),
+            )
+            a_n_codes[g] = codes_tile
+            a_n_scales[g] = scales_tile
+
+        def project(g, n):
+            if n == 0:
+                out_tile = work.tile([P, GROUP, O], F32)
+                out_sb[g] = out_tile
+            out_ps = ps_o.tile([P, O], F32)
+            nc.tensor.matmul_mx(
+                out=out_ps[:],
+                lhsT=a_n_codes[g][:, block(n)].bitcast(FP8X4),
+                lhsT_scale=a_n_scales[g][:, block(n)],
+                rhs=wv_codes[:].bitcast(FP8X4),
+                rhs_scale=wv_scales[:],
+                start=True,
+                stop=True,
+            )
+            if n == SCALAR_BANK:
+                nc.scalar.copy(out=out_sb[g][:, n, :], in_=out_ps[:])
+            else:
+                nc.vector.tensor_copy(out=out_sb[g][:, n, :], in_=out_ps[:])
+            if n == GROUP - 1:
+                nc.sync.dma_start(out=out_dram[:, g * GROUP : (g + 1) * GROUP, :], in_=out_sb[g][:])
+
+        transpose_actions(0)
+        for step in range(STEPS):
+            due = tile_due(step, 0)
+            if due is not None:
+                encode(due[0], due[1])
+            g = group_due(step, QUANTISE_LAG)
+            if g is not None:
+                quantise(g)
+            g = group_due(step, 1 - GROUP)
+            if g is not None:
+                transpose_actions(g)
+            due = tile_due(step, SQUARE_LAG)
+            if due is not None:
+                square(due[0], due[1])
+            g = group_due(step, DEVIATION_LAG)
+            if g is not None:
+                deviation(g)
+            due = tile_due(step, FLIP_LAG)
+            if due is not None:
+                flip(due[0], due[1])
+            due = tile_due(step, PROJECT_LAG)
+            if due is not None:
+                project(due[0], due[1])
+            g = group_due(step, REGROUP_LAG)
+            if g is not None:
+                regroup(g)
+            g = group_due(step, NORMALISE_LAG)
+            if g is not None:
+                normalise(g)
+            b = step - PREPARE_STEP
+            if b == 0:
+                transpose_gain_shift()
+            if 0 <= b < O // P:
+                transpose_wv(b)
+            if b == O // P:
+                quantise_wv()

@@ -29,9 +29,8 @@ SQUARE_LAG = 2
 DEVIATION_LAG = SQUARE_LAG + GROUP - 1
 NORMALISE_LAG = 6
 FLIP_LAG = 10
-REGROUP_LAG = 15
-QUANTISE_LAG = 16
-PROJECT_LAG = 17
+PACK_LAG = NORMALISE_LAG + 3 * GROUP
+PROJECT_LAG = PACK_LAG + 2
 STEPS = TILES + PROJECT_LAG
 SCALAR_BANK = 2
 PREPARE_STEP = 4
@@ -249,12 +248,14 @@ def tile_actionbindingattention_pa_kernel(tc, actions, W_ae, b_ae, ln_g, ln_b, W
 
         transpose_actions(0)
         for step in range(STEPS):
+            packed = group_due(step, PACK_LAG)
+            if packed is not None:
+                regroup(packed)
             due = tile_due(step, 0)
             if due is not None:
                 encode(due[0], due[1])
-            g = group_due(step, QUANTISE_LAG)
-            if g is not None:
-                quantise(g)
+            if packed is not None:
+                quantise(packed)
             g = group_due(step, 1 - GROUP)
             if g is not None:
                 transpose_actions(g)
@@ -270,9 +271,6 @@ def tile_actionbindingattention_pa_kernel(tc, actions, W_ae, b_ae, ln_g, ln_b, W
             due = tile_due(step, PROJECT_LAG)
             if due is not None:
                 project(due[0], due[1])
-            g = group_due(step, REGROUP_LAG)
-            if g is not None:
-                regroup(g)
             g = group_due(step, NORMALISE_LAG)
             if g is not None:
                 normalise(g)

@@ -32,7 +32,7 @@ FLIP_LAG = 10
 PACK_LAG = NORMALISE_LAG + 3 * GROUP
 PROJECT_LAG = PACK_LAG + 2
 STEPS = TILES + PROJECT_LAG
-SCALAR_BANK = 2
+SCALAR_BANKS = (1, 2)
 PREPARE_STEP = 4
 
 FLOPS = 2 * TOKENS * A * F + 2 * TOKENS * F * O
@@ -239,7 +239,7 @@ def tile_actionbindingattention_pa_kernel(tc, actions, W_ae, b_ae, ln_g, ln_b, W
                 start=True,
                 stop=True,
             )
-            if n == SCALAR_BANK:
+            if n in SCALAR_BANKS:
                 nc.scalar.copy(out=out_sb[g][:, n, :], in_=out_ps[:])
             else:
                 nc.vector.tensor_copy(out=out_sb[g][:, n, :], in_=out_ps[:])

@@ -61,6 +61,7 @@ def tile_actionbindingattention_pa_kernel(tc, actions, W_ae, b_ae, ln_g, ln_b, W
         keep = ctx.enter_context(tc.tile_pool(name="keep", bufs=1))
         work = ctx.enter_context(tc.tile_pool(name="work", bufs=3))
         small = ctx.enter_context(tc.tile_pool(name="small", bufs=4))
+        results = ctx.enter_context(tc.tile_pool(name="results", bufs=8))
         ps_bf = ctx.enter_context(tc.psum_pool(name="ps_bf", bufs=2))
         ps_a = ctx.enter_context(tc.psum_pool(name="ps_a", bufs=2))
         ps_z = ctx.enter_context(tc.psum_pool(name="ps_z", bufs=2))
@@ -69,11 +70,12 @@ def tile_actionbindingattention_pa_kernel(tc, actions, W_ae, b_ae, ln_g, ln_b, W
 
         w_ae_sb = keep.tile([P, PACK, A], BF16)
         nc.sync.dma_start(out=w_ae_sb[:], in_=W_ae.rearrange("(j p) a -> p j a", p=P))
+        bias_row = keep.tile([P, F], BF16)
+        nc.vector.memset(bias_row[:], 0.0)
+        nc.sync.dma_start(out=bias_row[0:1, :], in_=b_ae.rearrange("(o f) -> o f", o=1))
         x_all = keep.tile([P, TILES, A], BF16)
         chunk = TILES // LOAD_CHUNKS
         nc.sync.dma_start(out=x_all[:, 0:chunk, :], in_=x_dram[:, 0:chunk, :])
-        bias_bc = keep.tile([P, F], BF16)
-        nc.sync.dma_start(out=bias_bc[:], in_=b_ae.partition_broadcast(P))
         gain_shift_rows = keep.tile([P, P], BF16)
         nc.vector.memset(gain_shift_rows[:], 0.0)
         nc.sync.dma_start(out=gain_shift_rows[0:PACK, :], in_=ln_g.rearrange("(j p) -> j p", p=P))
@@ -88,14 +90,23 @@ def tile_actionbindingattention_pa_kernel(tc, actions, W_ae, b_ae, ln_g, ln_b, W
         make_identity(nc, ident_bf[:])
         ident_f32 = keep.tile([P, P], F32)
         make_identity(nc, ident_f32[:])
+        ones_bf = keep.tile([P, P], BF16)
+        nc.vector.memset(ones_bf[:], 1.0)
         eps = keep.tile([P, 1], F32)
         nc.vector.memset(eps[:], LN_EPS)
+        table_warmer = keep.tile([P, 1], F32)
+        nc.scalar.activation(out=table_warmer[:], in_=eps[:], func=ACT.Sqrt)
 
         w_aeT_ps = ps_bf.tile([P, F], BF16, tag="bf")
         for j in range(PACK):
             nc.tensor.transpose(out=w_aeT_ps[:, block(j)], in_=w_ae_sb[:, j, :], identity=ident_bf[:])
         w_aeT = keep.tile([P, F], BF16)
         nc.vector.tensor_copy(out=w_aeT[:], in_=w_aeT_ps[:])
+
+        bias_ps = ps_a.tile([P, F], F32, tag="a_ps")
+        nc.tensor.matmul(out=bias_ps[:], lhsT=ones_bf[:], rhs=bias_row[:], start=True, stop=True)
+        bias_bc = keep.tile([P, F], F32)
+        nc.vector.tensor_copy(out=bias_bc[:], in_=bias_ps[:])
 
         gain = keep.tile([P, PACK], F32)
         shift = keep.tile([P, PACK], F32)
@@ -123,7 +134,7 @@ def tile_actionbindingattention_pa_kernel(tc, actions, W_ae, b_ae, ln_g, ln_b, W
             )
 
         xT, a_sb, a_sum, dev_sq_sum, std, z_sb = {}, {}, {}, {}, {}, {}
-        a_n_planes, a_n_grouped, a_n_codes, a_n_scales, out_sb = {}, {}, {}, {}, {}
+        a_n_planes, a_n_grouped, a_n_codes, a_n_scales = {}, {}, {}, {}
 
         def transpose_actions(g):
             xT_ps = ps_bf.tile([P, GROUP_TOKENS], BF16, tag="bf")
@@ -226,9 +237,6 @@ def tile_actionbindingattention_pa_kernel(tc, actions, W_ae, b_ae, ln_g, ln_b, W
             a_n_scales[g] = scales_tile
 
         def project(g, n):
-            if n == 0:
-                out_tile = work.tile([P, GROUP, O], F32)
-                out_sb[g] = out_tile
             out_ps = ps_o.tile([P, O], F32)
             nc.tensor.matmul_mx(
                 out=out_ps[:],
@@ -239,12 +247,12 @@ def tile_actionbindingattention_pa_kernel(tc, actions, W_ae, b_ae, ln_g, ln_b, W
                 start=True,
                 stop=True,
             )
+            out_sb = results.tile([P, O], F32)
             if n in SCALAR_BANKS:
-                nc.scalar.copy(out=out_sb[g][:, n, :], in_=out_ps[:])
+                nc.scalar.copy(out=out_sb[:], in_=out_ps[:])
             else:
-                nc.vector.tensor_copy(out=out_sb[g][:, n, :], in_=out_ps[:])
-            if n == GROUP - 1:
-                nc.sync.dma_start(out=out_dram[:, g * GROUP : (g + 1) * GROUP, :], in_=out_sb[g][:])
+                nc.vector.tensor_copy(out=out_sb[:], in_=out_ps[:])
+            nc.sync.dma_start(out=out_dram[:, g * GROUP + n, :], in_=out_sb[:])
 
         transpose_actions(0)
         for step in range(STEPS):

from contextlib import ExitStack

import concourse.mybir as mybir
from concourse.masks import make_identity

BF16 = mybir.dt.bfloat16
F32 = mybir.dt.float32
U32 = mybir.dt.uint32
U8 = mybir.dt.uint8
FP8X4 = mybir.dt.float8_e4m3fn_x4
ACT = mybir.ActivationFunctionType
ALU = mybir.AluOpType

P = 128
PACK = 4
TOKENS = 64 * 128
A = 128
F = 512
O = 512
TILES = TOKENS // P
GROUP = 4
GROUPS = TILES // GROUP
GROUP_TOKENS = GROUP * P
LOAD_CHUNKS = 4
RUN = 4
LN_EPS = 1e-5

SQUARE_LAG = 2
DEVIATION_LAG = SQUARE_LAG + GROUP - 1
NORMALISE_LAG = 6
FLIP_LAG = 10
PACK_LAG = NORMALISE_LAG + 3 * GROUP
PROJECT_LAG = PACK_LAG + 2
STEPS = TILES + PROJECT_LAG
SCALAR_BANKS = (1, 2)
PREPARE_STEP = 4

FLOPS = 2 * TOKENS * A * F + 2 * TOKENS * F * O


def block(i):
    return slice(i * P, (i + 1) * P)


def tile_due(step, lag):
    k = step - lag
    return divmod(k, GROUP) if 0 <= k < TILES else None


def group_due(step, lag):
    due = tile_due(step, lag)
    return due[0] if due is not None and due[1] == 0 else None


def tile_actionbindingattention_pa_kernel(tc, actions, W_ae, b_ae, ln_g, ln_b, Wv, out):
    nc = tc.nc
    x_dram = actions.flatten_outer_dims().rearrange("(p n) a -> p n a", n=TILES)
    out_dram = out.flatten_outer_dims().rearrange("(p n) o -> p n o", n=TILES)

    with ExitStack() as ctx:
        keep = ctx.enter_context(tc.tile_pool(name="keep", bufs=1))
        work = ctx.enter_context(tc.tile_pool(name="work", bufs=3))
        small = ctx.enter_context(tc.tile_pool(name="small", bufs=4))
        results = ctx.enter_context(tc.tile_pool(name="results", bufs=8))
        ps_bf = ctx.enter_context(tc.psum_pool(name="ps_bf", bufs=2))
        ps_a = ctx.enter_context(tc.psum_pool(name="ps_a", bufs=2))
        ps_z = ctx.enter_context(tc.psum_pool(name="ps_z", bufs=2))
        ps_o = ctx.enter_context(tc.psum_pool(name="ps_o", bufs=2))
        ctx.enter_context(tc.manual_schedule())

        w_ae_sb = keep.tile([P, PACK, A], BF16)
        nc.sync.dma_start(out=w_ae_sb[:], in_=W_ae.rearrange("(j p) a -> p j a", p=P))
        bias_row = keep.tile([P, F], BF16)
        nc.vector.memset(bias_row[:], 0.0)
        nc.sync.dma_start(out=bias_row[0:1, :], in_=b_ae.rearrange("(o f) -> o f", o=1))
        x_all = keep.tile([P, TILES, A], BF16)
        chunk = TILES // LOAD_CHUNKS
        nc.sync.dma_start(out=x_all[:, 0:chunk, :], in_=x_dram[:, 0:chunk, :])
        gain_shift_rows = keep.tile([P, P], BF16)
        nc.vector.memset(gain_shift_rows[:], 0.0)
        nc.sync.dma_start(out=gain_shift_rows[0:PACK, :], in_=ln_g.rearrange("(j p) -> j p", p=P))
        nc.sync.dma_start(out=gain_shift_rows[PACK : 2 * PACK, :], in_=ln_b.rearrange("(j p) -> j p", p=P))
        wv_sb = keep.tile([P, O // P, F], BF16)
        nc.sync.dma_start(out=wv_sb[:], in_=Wv.rearrange("(b r) f -> r b f", r=P))
        for c in range(1, LOAD_CHUNKS):
            rows = slice(c * chunk, (c + 1) * chunk)
            nc.sync.dma_start(out=x_all[:, rows, :], in_=x_dram[:, rows, :])

        ident_bf = keep.tile([P, P], BF16)
        make_identity(nc, ident_bf[:])
        ident_f32 = keep.tile([P, P], F32)
        make_identity(nc, ident_f32[:])
        ones_bf = keep.tile([P, P], BF16)
        nc.vector.memset(ones_bf[:], 1.0)
        eps = keep.tile([P, 1], F32)
        nc.vector.memset(eps[:], LN_EPS)
        table_warmer = keep.tile([P, 1], F32)
        nc.scalar.activation(out=table_warmer[:], in_=eps[:], func=ACT.Sqrt)

        w_aeT_ps = ps_bf.tile([P, F], BF16, tag="bf")
        for j in range(PACK):
            nc.tensor.transpose(out=w_aeT_ps[:, block(j)], in_=w_ae_sb[:, j, :], identity=ident_bf[:])
        w_aeT = keep.tile([P, F], BF16)
        nc.vector.tensor_copy(out=w_aeT[:], in_=w_aeT_ps[:])

        bias_ps = ps_a.tile([P, F], F32, tag="a_ps")
        nc.tensor.matmul(out=bias_ps[:], lhsT=ones_bf[:], rhs=bias_row[:], start=True, stop=True)
        bias_bc = keep.tile([P, F], F32)
        nc.vector.tensor_copy(out=bias_bc[:], in_=bias_ps[:])

        gain = keep.tile([P, PACK], F32)
        shift = keep.tile([P, PACK], F32)
        wv_grouped = keep.tile([P, O, PACK], BF16, align_bytes=64)
        wv_codes = keep.tile([P, O], U32, align_bytes=64)
        wv_scales = keep.tile([P, O], U8, align_bytes=64)

        def transpose_gain_shift():
            gain_shift_ps = ps_bf.tile([P, P], BF16, tag="bf")
            nc.tensor.transpose(out=gain_shift_ps[:], in_=gain_shift_rows[:], identity=ident_bf[:])
            nc.vector.tensor_copy(out=gain[:], in_=gain_shift_ps[:, 0:PACK])
            nc.vector.tensor_copy(out=shift[:], in_=gain_shift_ps[:, PACK : 2 * PACK])

        def transpose_wv(b):
            wvT_ps = ps_bf.tile([P, PACK, P], BF16, tag="bf")
            for j in range(PACK):
                nc.tensor.transpose(out=wvT_ps[:, j, :], in_=wv_sb[:, b, block(j)], identity=ident_bf[:])
            nc.vector.tensor_copy(out=wv_grouped[:, block(b), :], in_=wvT_ps[:].rearrange("p j o -> p o j"))

        def quantise_wv():
            nc.vector.quantize_mx(
                out=wv_codes[:].bitcast(FP8X4),
                scales=wv_scales[:],
                in_=wv_grouped[:].rearrange("p o j -> p (o j)"),
            )

        xT, a_sb, a_sum, dev_sq_sum, std, z_sb = {}, {}, {}, {}, {}, {}
        a_n_planes, a_n_grouped, a_n_codes, a_n_scales = {}, {}, {}, {}

        def transpose_actions(g):
            xT_ps = ps_bf.tile([P, GROUP_TOKENS], BF16, tag="bf")
            for n in range(GROUP):
                nc.tensor.transpose(out=xT_ps[:, block(n)], in_=x_all[:, g * GROUP + n, :], identity=ident_bf[:])
            xT_sb = work.tile([P, GROUP_TOKENS], BF16)
            nc.scalar.copy(out=xT_sb[:], in_=xT_ps[:])
            xT[g] = xT_sb

        def encode(g, n):
            if n == 0:
                a_tile = work.tile([P, GROUP, F], F32)
                a_sb[g] = a_tile
                sum_tile = small.tile([P, GROUP], F32)
                a_sum[g] = sum_tile
            a_ps = ps_a.tile([P, F], F32)
            nc.tensor.matmul(out=a_ps[:], lhsT=xT[g][:, block(n)], rhs=w_aeT[:], start=True, stop=True)
            nc.vector.scalar_tensor_tensor(
                out=a_sb[g][:, n, :],
                in0=a_ps[:],
                scalar=1.0,
                in1=bias_bc[:],
                op0=ALU.mult,
                op1=ALU.add,
                accum_out=a_sum[g][:, n : n + 1],
            )

        def square(g, n):
            if n == 0:
                sq_tile = small.tile([P, GROUP], F32)
                dev_sq_sum[g] = sq_tile
            dev_sq = work.tile([P, F], BF16)
            nc.scalar.activation(
                out=dev_sq[:],
                in_=a_sb[g][:, n, :],
                func=ACT.Square,
                bias=a_sum[g][:, n : n + 1],
                scale=-1.0 * F,
                accum_out=dev_sq_sum[g][:, n : n + 1],
            )

        def deviation(g):
            std_tile = small.tile([P, GROUP], F32)
            nc.scalar.activation(
                out=std_tile[:], in_=dev_sq_sum[g][:], func=ACT.Sqrt, bias=eps[:], scale=1.0 / (F * F * F)
            )
            std[g] = std_tile

        def normalise(g):
            rstd = small.tile([P, GROUP], F32)
            nc.vector.reciprocal(out=rstd[:], in_=std[g][:])
            neg_mean_rstd = small.tile([P, GROUP], F32)
            nc.vector.scalar_tensor_tensor(
                out=neg_mean_rstd[:], in0=a_sum[g][:], scalar=-1.0 / F, in1=rstd[:], op0=ALU.mult, op1=ALU.mult
            )
            z_tile = work.tile([P, GROUP, F], F32)
            for n in range(GROUP):
                nc.gpsimd.tensor_scalar(
                    out=z_tile[:, n, :],
                    in0=a_sb[g][:, n, :],
                    scalar1=rstd[:, n : n + 1],
                    scalar2=neg_mean_rstd[:, n : n + 1],
                    op0=ALU.mult,
                    op1=ALU.add,
                )
            z_sb[g] = z_tile

        def flip(g, j):
            if j == 0:
                planes_tile = work.tile([P, PACK, GROUP_TOKENS], BF16)
                a_n_planes[g] = planes_tile
            zT_ps = ps_z.tile([P, GROUP_TOKENS], F32)
            for n in range(GROUP):
                nc.tensor.transpose(out=zT_ps[:, block(n)], in_=z_sb[g][:, n, block(j)], identity=ident_f32[:])
            nc.scalar.activation(
                out=a_n_planes[g][:, j, :],
                in_=zT_ps[:],
                func=ACT.Identity,
                scale=gain[:, j : j + 1],
                bias=shift[:, j : j + 1],
            )

        def regroup(g):
            grouped_tile = work.tile([P, GROUP_TOKENS, PACK], BF16, align_bytes=64)
            nc.vector.tensor_copy(
                out=grouped_tile[:].rearrange("p (c i) j -> p c j i", i=RUN),
                in_=a_n_planes[g][:].rearrange("p j (c i) -> p c j i", i=RUN),
            )
            a_n_grouped[g] = grouped_tile

        def quantise(g):
            codes_tile = work.tile([P, GROUP_TOKENS], U32, align_bytes=64)
            scales_tile = work.tile([P, GROUP_TOKENS], U8, align_bytes=64)
            nc.vector.quantize_mx(
                out=codes_tile[:].bitcast(FP8X4),
                scales=scales_tile[:],
                in_=a_n_grouped[g][:].rearrange("p c j -> p (c j)"),
            )
            a_n_codes[g] = codes_tile
            a_n_scales[g] = scales_tile

        def project(g, n):
            out_ps = ps_o.tile([P, O], F32)
            nc.tensor.matmul_mx(
                out=out_ps[:],
                lhsT=a_n_codes[g][:, block(n)].bitcast(FP8X4),
                lhsT_scale=a_n_scales[g][:, block(n)],
                rhs=wv_codes[:].bitcast(FP8X4),
                rhs_scale=wv_scales[:],
                start=True,
                stop=True,
            )
            out_sb = results.tile([P, O], F32)
            if n in SCALAR_BANKS:
                nc.scalar.copy(out=out_sb[:], in_=out_ps[:])
            else:
                nc.vector.tensor_copy(out=out_sb[:], in_=out_ps[:])
            nc.sync.dma_start(out=out_dram[:, g * GROUP + n, :], in_=out_sb[:])

        transpose_actions(0)
        for step in range(STEPS):
            packed = group_due(step, PACK_LAG)
            if packed is not None:
                regroup(packed)
            due = tile_due(step, 0)
            if due is not None:
                encode(due[0], due[1])
            if packed is not None:
                quantise(packed)
            g = group_due(step, 1 - GROUP)
            if g is not None:
                transpose_actions(g)
            due = tile_due(step, SQUARE_LAG)
            if due is not None:
                square(due[0], due[1])
            g = group_due(step, DEVIATION_LAG)
            if g is not None:
                deviation(g)
            due = tile_due(step, FLIP_LAG)
            if due is not None:
                flip(due[0], due[1])
            due = tile_due(step, PROJECT_LAG)
            if due is not None:
                project(due[0], due[1])
            g = group_due(step, NORMALISE_LAG)
            if g is not None:
                normalise(g)
            b = step - PREPARE_STEP
            if b == 0:
                transpose_gain_shift()
            if 0 <= b < O // P:
                transpose_wv(b)
            if b == O // P:
                quantise_wv()
